import numpy as np
import ml_dtypes

BF16 = ml_dtypes.bfloat16


def bf(x):
    return np.asarray(x, np.float32).astype(BF16)


def f32(x):
    return np.asarray(x, np.float32)


def f64(x):
    return np.asarray(x).astype(np.float64)


def striped(idx):
    return np.tile(idx.reshape(-1, 16).T, (8, 1))


C, S, K, N, KEEP, GM = 128, 256, 8, 2048, 2, 4


def sparse_weight():
    raw = np.random.standard_normal((C, S))
    grp = np.abs(raw).reshape(-1, GM)
    order = np.argsort(grp, axis=-1)
    keep = np.zeros(grp.shape, bool)
    np.put_along_axis(keep, order[:, -KEEP:], True, axis=-1)
    return raw * keep.reshape(C, S)


def setup_inputs():
    x = bf(sparse_weight())
    lead = np.concatenate([np.ones((1, S)), np.zeros((K - 1, S))], 0)
    c1 = bf((lead + 0.2 * np.random.standard_normal((K, S))).reshape(1, N))
    c0 = f32(1.0 + 0.1 * np.random.standard_normal((C, 1)))
    idx = np.concatenate([np.random.permutation(S) for _ in range(K)])
    return {"x": x, "c1": c1, "c0": c0, "offs": striped(idx)}


def reference(x, c1, c0, offs):
    idx = offs[:16].T.reshape(-1)
    prod = f64(x)[:, idx] * f64(c1)
    return f64(c0) * prod.reshape(C, K, S).sum(axis=1)

@@ -1,0 +1,43 @@
+import concourse.mybir as mybir
+
+C = 128
+S = 256
+K = 8
+N = K * S
+COLS = S // 16
+
+BF16, F32, U16 = mybir.dt.bfloat16, mybir.dt.float32, mybir.dt.uint16
+MULT = mybir.AluOpType.mult
+
+
+def tile_permutedsparseweight_kernel(tc, x, c1, c0, offs, out):
+    nc = tc.nc
+    with (
+        tc.tile_pool(name="held", bufs=1) as held,
+        tc.tile_pool(name="pieces", bufs=K) as pieces,
+    ):
+        offsets = held.tile([C, N // 16], U16, name="offsets")
+        nc.sync.dma_start(offsets[:], offs)
+        x_bf16 = held.tile([C, S], BF16, name="x_bf16")
+        nc.scalar.dma_start(x_bf16[:], x)
+        gain = held.tile([C, 1], F32, name="gain")
+        nc.scalar.dma_start(gain[:], c0)
+
+        window = held.tile([C, S], F32, name="window")
+        nc.vector.tensor_copy(window[:], x_bf16[:])
+
+        total = held.tile([C, S], F32, name="total")
+        for p in range(K):
+            coef_bf16 = pieces.tile([C, S], BF16, name="coef_bf16")
+            nc.sync.dma_start(coef_bf16[:], c1[:, p * S : (p + 1) * S].broadcast_to([C, S]))
+            coef = pieces.tile([C, S], F32, name="coef")
+            nc.scalar.mul(coef[:], coef_bf16[:], gain[:, 0:1])
+            picked = window[:].indirect(offsets[:, p * COLS : (p + 1) * COLS])
+            if p == 0:
+                nc.vector.tensor_tensor(total[:], picked, coef[:], MULT)
+            else:
+                product = pieces.tile([C, S], F32, name="product")
+                nc.vector.tensor_tensor(product[:], picked, coef[:], MULT)
+                nc.vector.tensor_add(total[:], total[:], product[:])
+
+        nc.sync.dma_start(out, total[:])

@@ -23,6 +23,10 @@ def tile_permutedsparseweight_kernel(tc, x, c1, c0, offs, out):
         gain = held.tile([C, 1], F32, name="gain")
         nc.scalar.dma_start(gain[:], c0)
 
+        scratch = held.tile([C, 1], F32, name="scratch")
+        nc.vector.memset(scratch[:], 0.0)
+        nc.scalar.mul(scratch[:], scratch[:], 1.0)
+
         window = held.tile([C, S], F32, name="window")
         nc.vector.tensor_copy(window[:], x_bf16[:])
 

@@ -1,4 +1,5 @@
 import concourse.mybir as mybir
+from concourse.masks import make_identity
 
 C = 128
 S = 256
@@ -7,7 +8,7 @@ N = K * S
 COLS = S // 16
 
 BF16, F32, U16 = mybir.dt.bfloat16, mybir.dt.float32, mybir.dt.uint16
-MULT = mybir.AluOpType.mult
+MULT, ADD = mybir.AluOpType.mult, mybir.AluOpType.add
 
 
 def tile_permutedsparseweight_kernel(tc, x, c1, c0, offs, out):
@@ -15,6 +16,7 @@ def tile_permutedsparseweight_kernel(tc, x, c1, c0, offs, out):
     with (
         tc.tile_pool(name="held", bufs=1) as held,
         tc.tile_pool(name="pieces", bufs=K) as pieces,
+        tc.psum_pool(name="psum", bufs=1) as psum,
     ):
         offsets = held.tile([C, N // 16], U16, name="offsets")
         nc.sync.dma_start(offsets[:], offs)
@@ -30,18 +32,21 @@ def tile_permutedsparseweight_kernel(tc, x, c1, c0, offs, out):
         window = held.tile([C, S], F32, name="window")
         nc.vector.tensor_copy(window[:], x_bf16[:])
 
-        total = held.tile([C, S], F32, name="total")
+        identity = held.tile([C, C], F32, name="identity")
+        make_identity(nc, identity[:])
+        partial = psum.tile([C, S], F32, name="partial")
+
         for p in range(K):
             coef_bf16 = pieces.tile([C, S], BF16, name="coef_bf16")
             nc.sync.dma_start(coef_bf16[:], c1[:, p * S : (p + 1) * S].broadcast_to([C, S]))
             coef = pieces.tile([C, S], F32, name="coef")
             nc.scalar.mul(coef[:], coef_bf16[:], gain[:, 0:1])
             picked = window[:].indirect(offsets[:, p * COLS : (p + 1) * COLS])
-            if p == 0:
-                nc.vector.tensor_tensor(total[:], picked, coef[:], MULT)
-            else:
-                product = pieces.tile([C, S], F32, name="product")
-                nc.vector.tensor_tensor(product[:], picked, coef[:], MULT)
-                nc.vector.tensor_add(total[:], total[:], product[:])
+            product = pieces.tile([C, S], F32, name="product")
+            nc.vector.tensor_tensor(product[:], picked, coef[:], MULT)
+            if p < K - 1:
+                nc.tensor.matmul(partial[:], identity[:], product[:], start=(p == 0), stop=(p == K - 2))
 
+        total = held.tile([C, S], F32, name="total")
+        nc.vector.tensor_tensor(total[:], product[:], partial[:], ADD)
         nc.sync.dma_start(out, total[:])

@@ -5,6 +5,7 @@ C = 128
 S = 256
 K = 8
 N = K * S
+K_TENSOR = K - 2
 COLS = S // 16
 
 BF16, F32, U16 = mybir.dt.bfloat16, mybir.dt.float32, mybir.dt.uint16
@@ -36,6 +37,7 @@ def tile_permutedsparseweight_kernel(tc, x, c1, c0, offs, out):
         make_identity(nc, identity[:])
         partial = psum.tile([C, S], F32, name="partial")
 
+        products = []
         for p in range(K):
             coef_bf16 = pieces.tile([C, S], BF16, name="coef_bf16")
             nc.sync.dma_start(coef_bf16[:], c1[:, p * S : (p + 1) * S].broadcast_to([C, S]))
@@ -44,9 +46,11 @@ def tile_permutedsparseweight_kernel(tc, x, c1, c0, offs, out):
             picked = window[:].indirect(offsets[:, p * COLS : (p + 1) * COLS])
             product = pieces.tile([C, S], F32, name="product")
             nc.vector.tensor_tensor(product[:], picked, coef[:], MULT)
-            if p < K - 1:
-                nc.tensor.matmul(partial[:], identity[:], product[:], start=(p == 0), stop=(p == K - 2))
+            products.append(product)
+            if p < K_TENSOR:
+                nc.tensor.matmul(partial[:], identity[:], product[:], start=(p == 0), stop=(p == K_TENSOR - 1))
 
         total = held.tile([C, S], F32, name="total")
-        nc.vector.tensor_tensor(total[:], product[:], partial[:], ADD)
+        nc.vector.tensor_tensor(total[:], products[K - 2][:], products[K - 1][:], ADD)
+        nc.vector.tensor_tensor(total[:], total[:], partial[:], ADD)
         nc.sync.dma_start(out, total[:])

@@ -9,7 +9,7 @@ K_TENSOR = K - 2
 COLS = S // 16
 
 BF16, F32, U16 = mybir.dt.bfloat16, mybir.dt.float32, mybir.dt.uint16
-MULT, ADD = mybir.AluOpType.mult, mybir.AluOpType.add
+MULT, ADD, NOT_EQUAL = mybir.AluOpType.mult, mybir.AluOpType.add, mybir.AluOpType.not_equal
 
 
 def tile_permutedsparseweight_kernel(tc, x, c1, c0, offs, out):
@@ -17,35 +17,47 @@ def tile_permutedsparseweight_kernel(tc, x, c1, c0, offs, out):
     with (
         tc.tile_pool(name="held", bufs=1) as held,
         tc.tile_pool(name="pieces", bufs=K) as pieces,
-        tc.psum_pool(name="psum", bufs=1) as psum,
+        tc.psum_pool(name="spread_banks", bufs=6) as spread_banks,
+        tc.psum_pool(name="sum_bank", bufs=1) as sum_bank,
     ):
+        c1_rows = held.tile([K, S], BF16, name="c1_rows")
+        nc.sync.dma_start(c1_rows[:], c1.rearrange("o (p s) -> (o p) s", p=K))
         offsets = held.tile([C, N // 16], U16, name="offsets")
         nc.sync.dma_start(offsets[:], offs)
-        x_bf16 = held.tile([C, S], BF16, name="x_bf16")
-        nc.scalar.dma_start(x_bf16[:], x)
         gain = held.tile([C, 1], F32, name="gain")
         nc.scalar.dma_start(gain[:], c0)
+        x_bf16 = held.tile([C, S], BF16, name="x_bf16")
+        nc.scalar.dma_start(x_bf16[:], x)
 
         scratch = held.tile([C, 1], F32, name="scratch")
         nc.vector.memset(scratch[:], 0.0)
         nc.scalar.mul(scratch[:], scratch[:], 1.0)
 
+        pick = held.tile([K, K], BF16, name="pick")
+        nc.gpsimd.memset(pick[:], 0.0)
+        nc.gpsimd.affine_select(
+            out=pick[:], in_=pick[:], compare_op=NOT_EQUAL, fill=1.0, base=0, pattern=[[-1, K]], channel_multiplier=1
+        )
+        identity = held.tile([C, C], F32, name="identity")
+        make_identity(nc, identity[:])
+
         window = held.tile([C, S], F32, name="window")
         nc.vector.tensor_copy(window[:], x_bf16[:])
 
-        identity = held.tile([C, C], F32, name="identity")
-        make_identity(nc, identity[:])
-        partial = psum.tile([C, S], F32, name="partial")
+        coefs = []
+        for p in range(K):
+            spread = spread_banks.tile([C, S], F32, name="spread")
+            nc.tensor.matmul(spread[:], pick[:, p : p + 1].to_broadcast([K, C]), c1_rows[:], start=True, stop=True)
+            coef = pieces.tile([C, S], F32, name="coef")
+            nc.scalar.mul(coef[:], spread[:], gain[:, 0:1])
+            coefs.append(coef)
 
+        partial = sum_bank.tile([C, S], F32, name="partial")
         products = []
         for p in range(K):
-            coef_bf16 = pieces.tile([C, S], BF16, name="coef_bf16")
-            nc.sync.dma_start(coef_bf16[:], c1[:, p * S : (p + 1) * S].broadcast_to([C, S]))
-            coef = pieces.tile([C, S], F32, name="coef")
-            nc.scalar.mul(coef[:], coef_bf16[:], gain[:, 0:1])
             picked = window[:].indirect(offsets[:, p * COLS : (p + 1) * COLS])
             product = pieces.tile([C, S], F32, name="product")
-            nc.vector.tensor_tensor(product[:], picked, coef[:], MULT)
+            nc.vector.tensor_tensor(product[:], picked, coefs[p][:], MULT)
             products.append(product)
             if p < K_TENSOR:
                 nc.tensor.matmul(partial[:], identity[:], product[:], start=(p == 0), stop=(p == K_TENSOR - 1))

@@ -7,6 +7,8 @@ K = 8
 N = K * S
 K_TENSOR = K - 2
 COLS = S // 16
+ROWS = 32
+RUN = N // ROWS
 
 BF16, F32, U16 = mybir.dt.bfloat16, mybir.dt.float32, mybir.dt.uint16
 MULT, ADD, NOT_EQUAL = mybir.AluOpType.mult, mybir.AluOpType.add, mybir.AluOpType.not_equal
@@ -20,8 +22,8 @@ def tile_permutedsparseweight_kernel(tc, x, c1, c0, offs, out):
         tc.psum_pool(name="spread_banks", bufs=6) as spread_banks,
         tc.psum_pool(name="sum_bank", bufs=1) as sum_bank,
     ):
-        c1_rows = held.tile([K, S], BF16, name="c1_rows")
-        nc.sync.dma_start(c1_rows[:], c1.rearrange("o (p s) -> (o p) s", p=K))
+        c1_rows = held.tile([C, RUN], BF16, name="c1_rows")
+        nc.sync.dma_start(c1_rows[0:ROWS, :], c1.rearrange("o (r t) -> (o r) t", r=ROWS))
         offsets = held.tile([C, N // 16], U16, name="offsets")
         nc.sync.dma_start(offsets[:], offs)
         gain = held.tile([C, 1], F32, name="gain")
@@ -32,11 +34,13 @@ def tile_permutedsparseweight_kernel(tc, x, c1, c0, offs, out):
         scratch = held.tile([C, 1], F32, name="scratch")
         nc.vector.memset(scratch[:], 0.0)
         nc.scalar.mul(scratch[:], scratch[:], 1.0)
+        nc.vector.memset(c1_rows[32:64, :], 0.0)
+        nc.vector.memset(c1_rows[64:128, :], 0.0)
 
-        pick = held.tile([K, K], BF16, name="pick")
+        pick = held.tile([C, ROWS], BF16, name="pick")
         nc.gpsimd.memset(pick[:], 0.0)
         nc.gpsimd.affine_select(
-            out=pick[:], in_=pick[:], compare_op=NOT_EQUAL, fill=1.0, base=0, pattern=[[-1, K]], channel_multiplier=1
+            out=pick[:], in_=pick[:], compare_op=NOT_EQUAL, fill=1.0, base=0, pattern=[[-1, ROWS]], channel_multiplier=1
         )
         identity = held.tile([C, C], F32, name="identity")
         make_identity(nc, identity[:])
@@ -47,7 +51,15 @@ def tile_permutedsparseweight_kernel(tc, x, c1, c0, offs, out):
         coefs = []
         for p in range(K):
             spread = spread_banks.tile([C, S], F32, name="spread")
-            nc.tensor.matmul(spread[:], pick[:, p : p + 1].to_broadcast([K, C]), c1_rows[:], start=True, stop=True)
+            for q in range(S // RUN):
+                r = p * (S // RUN) + q
+                nc.tensor.matmul(
+                    spread[:, q * RUN : (q + 1) * RUN],
+                    pick[:, r : r + 1].to_broadcast([C, C]),
+                    c1_rows[:],
+                    start=True,
+                    stop=True,
+                )
             coef = pieces.tile([C, S], F32, name="coef")
             nc.scalar.mul(coef[:], spread[:], gain[:, 0:1])
             coefs.append(coef)

@@ -5,7 +5,7 @@ C = 128
 S = 256
 K = 8
 N = K * S
-K_TENSOR = K - 2
+K_TENSOR = K - 1
 COLS = S // 16
 ROWS = 32
 RUN = N // ROWS
@@ -75,6 +75,5 @@ def tile_permutedsparseweight_kernel(tc, x, c1, c0, offs, out):
                 nc.tensor.matmul(partial[:], identity[:], product[:], start=(p == 0), stop=(p == K_TENSOR - 1))
 
         total = held.tile([C, S], F32, name="total")
-        nc.vector.tensor_tensor(total[:], products[K - 2][:], products[K - 1][:], ADD)
-        nc.vector.tensor_tensor(total[:], total[:], partial[:], ADD)
+        nc.vector.tensor_tensor(total[:], products[K - 1][:], partial[:], ADD)
         nc.sync.dma_start(out, total[:])

@@ -26,10 +26,10 @@ def tile_permutedsparseweight_kernel(tc, x, c1, c0, offs, out):
         nc.sync.dma_start(c1_rows[0:ROWS, :], c1.rearrange("o (r t) -> (o r) t", r=ROWS))
         offsets = held.tile([C, N // 16], U16, name="offsets")
         nc.sync.dma_start(offsets[:], offs)
-        gain = held.tile([C, 1], F32, name="gain")
-        nc.scalar.dma_start(gain[:], c0)
         x_bf16 = held.tile([C, S], BF16, name="x_bf16")
         nc.scalar.dma_start(x_bf16[:], x)
+        gain = held.tile([C, 1], F32, name="gain")
+        nc.scalar.dma_start(gain[:], c0)
 
         scratch = held.tile([C, 1], F32, name="scratch")
         nc.vector.memset(scratch[:], 0.0)
@@ -61,7 +61,10 @@ def tile_permutedsparseweight_kernel(tc, x, c1, c0, offs, out):
                     stop=True,
                 )
             coef = pieces.tile([C, S], F32, name="coef")
-            nc.scalar.mul(coef[:], spread[:], gain[:, 0:1])
+            if p == 0:
+                nc.vector.tensor_copy(coef[:], spread[:])
+            else:
+                nc.scalar.mul(coef[:], spread[:], 1.0 if p < K_TENSOR else gain[:, 0:1])
             coefs.append(coef)
 
         partial = sum_bank.tile([C, S], F32, name="partial")
@@ -75,5 +78,5 @@ def tile_permutedsparseweight_kernel(tc, x, c1, c0, offs, out):
                 nc.tensor.matmul(partial[:], identity[:], product[:], start=(p == 0), stop=(p == K_TENSOR - 1))
 
         total = held.tile([C, S], F32, name="total")
-        nc.vector.tensor_tensor(total[:], products[K - 1][:], partial[:], ADD)
+        nc.vector.scalar_tensor_tensor(total[:], partial[:], gain[:, 0:1], products[K - 1][:], MULT, ADD)
         nc.sync.dma_start(out, total[:])

@@ -14,6 +14,11 @@ BF16, F32, U16 = mybir.dt.bfloat16, mybir.dt.float32, mybir.dt.uint16
 MULT, ADD, NOT_EQUAL = mybir.AluOpType.mult, mybir.AluOpType.add, mybir.AluOpType.not_equal
 
 
+def cuts(p):
+    parts = 2 if p == K_TENSOR - 1 else 1
+    return [(h * (S // parts), S // parts) for h in range(parts)]
+
+
 def tile_permutedsparseweight_kernel(tc, x, c1, c0, offs, out):
     nc = tc.nc
     with (
@@ -70,12 +75,20 @@ def tile_permutedsparseweight_kernel(tc, x, c1, c0, offs, out):
         partial = sum_bank.tile([C, S], F32, name="partial")
         products = []
         for p in range(K):
-            picked = window[:].indirect(offsets[:, p * COLS : (p + 1) * COLS])
             product = pieces.tile([C, S], F32, name="product")
-            nc.vector.tensor_tensor(product[:], picked, coefs[p][:], MULT)
             products.append(product)
-            if p < K_TENSOR:
-                nc.tensor.matmul(partial[:], identity[:], product[:], start=(p == 0), stop=(p == K_TENSOR - 1))
+            for first, width in cuts(p):
+                columns = slice(first, first + width)
+                picked = window[:].indirect(offsets[:, p * COLS + first // 16 : p * COLS + (first + width) // 16])
+                nc.vector.tensor_tensor(product[:, columns], picked, coefs[p][:, columns], MULT)
+                if p < K_TENSOR:
+                    nc.tensor.matmul(
+                        partial[:, columns],
+                        identity[:],
+                        product[:, columns],
+                        start=(p == 0),
+                        stop=(p == K_TENSOR - 1 and first + width == S),
+                    )
 
         total = held.tile([C, S], F32, name="total")
         nc.vector.scalar_tensor_tensor(total[:], partial[:], gain[:, 0:1], products[K - 1][:], MULT, ADD)

@@ -7,11 +7,9 @@ K = 8
 N = K * S
 K_TENSOR = K - 1
 COLS = S // 16
-ROWS = 32
-RUN = N // ROWS
 
 BF16, F32, U16 = mybir.dt.bfloat16, mybir.dt.float32, mybir.dt.uint16
-MULT, ADD, NOT_EQUAL = mybir.AluOpType.mult, mybir.AluOpType.add, mybir.AluOpType.not_equal
+MULT, ADD = mybir.AluOpType.mult, mybir.AluOpType.add
 
 
 def cuts(p):
@@ -27,8 +25,8 @@ def tile_permutedsparseweight_kernel(tc, x, c1, c0, offs, out):
         tc.psum_pool(name="spread_banks", bufs=6) as spread_banks,
         tc.psum_pool(name="sum_bank", bufs=1) as sum_bank,
     ):
-        c1_rows = held.tile([C, RUN], BF16, name="c1_rows")
-        nc.sync.dma_start(c1_rows[0:ROWS, :], c1.rearrange("o (r t) -> (o r) t", r=ROWS))
+        c1_row = held.tile([C, N], BF16, name="c1_row")
+        nc.sync.dma_start(c1_row[C - 1 : C, :], c1)
         offsets = held.tile([C, N // 16], U16, name="offsets")
         nc.sync.dma_start(offsets[:], offs)
         x_bf16 = held.tile([C, S], BF16, name="x_bf16")
@@ -39,14 +37,10 @@ def tile_permutedsparseweight_kernel(tc, x, c1, c0, offs, out):
         scratch = held.tile([C, 1], F32, name="scratch")
         nc.vector.memset(scratch[:], 0.0)
         nc.scalar.mul(scratch[:], scratch[:], 1.0)
-        nc.vector.memset(c1_rows[32:64, :], 0.0)
-        nc.vector.memset(c1_rows[64:128, :], 0.0)
+        ones = held.tile([C, C], BF16, name="ones")
+        nc.vector.memset(ones[:], 1.0)
+        nc.vector.memset(c1_row[0 : C - 1, :], 0.0)
 
-        pick = held.tile([C, ROWS], BF16, name="pick")
-        nc.gpsimd.memset(pick[:], 0.0)
-        nc.gpsimd.affine_select(
-            out=pick[:], in_=pick[:], compare_op=NOT_EQUAL, fill=1.0, base=0, pattern=[[-1, ROWS]], channel_multiplier=1
-        )
         identity = held.tile([C, C], F32, name="identity")
         make_identity(nc, identity[:])
 
@@ -56,15 +50,7 @@ def tile_permutedsparseweight_kernel(tc, x, c1, c0, offs, out):
         coefs = []
         for p in range(K):
             spread = spread_banks.tile([C, S], F32, name="spread")
-            for q in range(S // RUN):
-                r = p * (S // RUN) + q
-                nc.tensor.matmul(
-                    spread[:, q * RUN : (q + 1) * RUN],
-                    pick[:, r : r + 1].to_broadcast([C, C]),
-                    c1_rows[:],
-                    start=True,
-                    stop=True,
-                )
+            nc.tensor.matmul(spread[:], ones[:], c1_row[:, p * S : (p + 1) * S], start=True, stop=True)
             coef = pieces.tile([C, S], F32, name="coef")
             if p == 0:
                 nc.vector.tensor_copy(coef[:], spread[:])

@@ -9,7 +9,7 @@ K_TENSOR = K - 1
 COLS = S // 16
 
 BF16, F32, U16 = mybir.dt.bfloat16, mybir.dt.float32, mybir.dt.uint16
-MULT, ADD = mybir.AluOpType.mult, mybir.AluOpType.add
+MULT, ADD, NOT_EQUAL = mybir.AluOpType.mult, mybir.AluOpType.add, mybir.AluOpType.not_equal
 
 
 def cuts(p):
@@ -25,8 +25,8 @@ def tile_permutedsparseweight_kernel(tc, x, c1, c0, offs, out):
         tc.psum_pool(name="spread_banks", bufs=6) as spread_banks,
         tc.psum_pool(name="sum_bank", bufs=1) as sum_bank,
     ):
-        c1_row = held.tile([C, N], BF16, name="c1_row")
-        nc.sync.dma_start(c1_row[C - 1 : C, :], c1)
+        c1_rows = held.tile([C, S], BF16, name="c1_rows")
+        nc.sync.dma_start(c1_rows[C - K : C, :], c1.rearrange("o (p s) -> (o p) s", p=K))
         offsets = held.tile([C, N // 16], U16, name="offsets")
         nc.sync.dma_start(offsets[:], offs)
         x_bf16 = held.tile([C, S], BF16, name="x_bf16")
@@ -37,9 +37,19 @@ def tile_permutedsparseweight_kernel(tc, x, c1, c0, offs, out):
         scratch = held.tile([C, 1], F32, name="scratch")
         nc.vector.memset(scratch[:], 0.0)
         nc.scalar.mul(scratch[:], scratch[:], 1.0)
-        ones = held.tile([C, C], BF16, name="ones")
-        nc.vector.memset(ones[:], 1.0)
-        nc.vector.memset(c1_row[0 : C - 1, :], 0.0)
+        nc.vector.memset(c1_rows[0 : C - K, :], 0.0)
+
+        pick = held.tile([C, K], BF16, name="pick")
+        nc.gpsimd.memset(pick[:], 0.0)
+        nc.gpsimd.affine_select(
+            out=pick[:],
+            in_=pick[:],
+            compare_op=NOT_EQUAL,
+            fill=1.0,
+            base=K - C,
+            pattern=[[-1, K]],
+            channel_multiplier=1,
+        )
 
         identity = held.tile([C, C], F32, name="identity")
         make_identity(nc, identity[:])
@@ -50,7 +60,7 @@ def tile_permutedsparseweight_kernel(tc, x, c1, c0, offs, out):
         coefs = []
         for p in range(K):
             spread = spread_banks.tile([C, S], F32, name="spread")
-            nc.tensor.matmul(spread[:], ones[:], c1_row[:, p * S : (p + 1) * S], start=True, stop=True)
+            nc.tensor.matmul(spread[:], pick[:, p : p + 1].to_broadcast([C, C]), c1_rows[:], start=True, stop=True)
             coef = pieces.tile([C, S], F32, name="coef")
             if p == 0:
                 nc.vector.tensor_copy(coef[:], spread[:])

@@ -12,9 +12,20 @@ BF16, F32, U16 = mybir.dt.bfloat16, mybir.dt.float32, mybir.dt.uint16
 MULT, ADD, NOT_EQUAL = mybir.AluOpType.mult, mybir.AluOpType.add, mybir.AluOpType.not_equal
 
 
-def cuts(p):
-    parts = 2 if p == K_TENSOR - 1 else 1
+def cut(parts):
     return [(h * (S // parts), S // parts) for h in range(parts)]
+
+
+def spread_cuts(p):
+    return cut(2 if p == 0 else 1)
+
+
+def add_cuts(p):
+    return cut(2 if p == K_TENSOR - 1 else 1)
+
+
+def look_up_cuts(p):
+    return cut(max(len(spread_cuts(p)), len(add_cuts(p))))
 
 
 def tile_permutedsparseweight_kernel(tc, x, c1, c0, offs, out):
@@ -59,25 +70,31 @@ def tile_permutedsparseweight_kernel(tc, x, c1, c0, offs, out):
 
         coefs = []
         for p in range(K):
-            spread = spread_banks.tile([C, S], F32, name="spread")
-            nc.tensor.matmul(spread[:], pick[:, p : p + 1].to_broadcast([C, C]), c1_rows[:], start=True, stop=True)
             coef = pieces.tile([C, S], F32, name="coef")
-            if p == 0:
-                nc.vector.tensor_copy(coef[:], spread[:])
-            else:
-                nc.scalar.mul(coef[:], spread[:], 1.0 if p < K_TENSOR else gain[:, 0:1])
             coefs.append(coef)
+            for first, width in spread_cuts(p):
+                columns = slice(first, first + width)
+                spread = spread_banks.tile([C, width], F32, name="spread")
+                nc.tensor.matmul(
+                    spread[:], pick[:, p : p + 1].to_broadcast([C, C]), c1_rows[:, columns], start=True, stop=True
+                )
+                if p == 0 and first == 0:
+                    nc.vector.tensor_copy(coef[:, columns], spread[:])
+                else:
+                    nc.scalar.mul(coef[:, columns], spread[:], 1.0 if p < K_TENSOR else gain[:, 0:1])
 
         partial = sum_bank.tile([C, S], F32, name="partial")
         products = []
         for p in range(K):
             product = pieces.tile([C, S], F32, name="product")
             products.append(product)
-            for first, width in cuts(p):
+            for first, width in look_up_cuts(p):
                 columns = slice(first, first + width)
                 picked = window[:].indirect(offsets[:, p * COLS + first // 16 : p * COLS + (first + width) // 16])
                 nc.vector.tensor_tensor(product[:, columns], picked, coefs[p][:, columns], MULT)
-                if p < K_TENSOR:
+            if p < K_TENSOR:
+                for first, width in add_cuts(p):
+                    columns = slice(first, first + width)
                     nc.tensor.matmul(
                         partial[:, columns],
                         identity[:],

@@ -5,7 +5,7 @@ C = 128
 S = 256
 K = 8
 N = K * S
-K_TENSOR = K - 1
+K_TENSOR = K - 2
 COLS = S // 16
 
 BF16, F32, U16 = mybir.dt.bfloat16, mybir.dt.float32, mybir.dt.uint16
@@ -18,14 +18,6 @@ def cut(parts):
 
 def spread_cuts(p):
     return cut(2 if p == 0 else 1)
-
-
-def add_cuts(p):
-    return cut(2 if p == K_TENSOR - 1 else 1)
-
-
-def look_up_cuts(p):
-    return cut(max(len(spread_cuts(p)), len(add_cuts(p))))
 
 
 def tile_permutedsparseweight_kernel(tc, x, c1, c0, offs, out):
@@ -84,25 +76,25 @@ def tile_permutedsparseweight_kernel(tc, x, c1, c0, offs, out):
                     nc.scalar.mul(coef[:, columns], spread[:], 1.0 if p < K_TENSOR else gain[:, 0:1])
 
         partial = sum_bank.tile([C, S], F32, name="partial")
+        scaled = held.tile([C, S], F32, name="scaled")
         products = []
         for p in range(K):
             product = pieces.tile([C, S], F32, name="product")
             products.append(product)
-            for first, width in look_up_cuts(p):
+            for first, width in spread_cuts(p):
                 columns = slice(first, first + width)
                 picked = window[:].indirect(offsets[:, p * COLS + first // 16 : p * COLS + (first + width) // 16])
                 nc.vector.tensor_tensor(product[:, columns], picked, coefs[p][:, columns], MULT)
             if p < K_TENSOR:
-                for first, width in add_cuts(p):
-                    columns = slice(first, first + width)
-                    nc.tensor.matmul(
-                        partial[:, columns],
-                        identity[:],
-                        product[:, columns],
-                        start=(p == 0),
-                        stop=(p == K_TENSOR - 1 and first + width == S),
-                    )
+                nc.tensor.matmul(partial[:], identity[:], product[:], start=(p == 0), stop=(p == K_TENSOR - 1))
 
         total = held.tile([C, S], F32, name="total")
-        nc.vector.scalar_tensor_tensor(total[:], partial[:], gain[:, 0:1], products[K - 1][:], MULT, ADD)
+        for first, width in cut(2):
+            columns = slice(first, first + width)
+            nc.vector.scalar_tensor_tensor(
+                scaled[:, columns], partial[:, columns], gain[:, 0:1], products[K - 2][:, columns], MULT, ADD
+            )
+        for first, width in cut(2):
+            columns = slice(first, first + width)
+            nc.vector.tensor_tensor(total[:, columns], scaled[:, columns], products[K - 1][:, columns], ADD)
         nc.sync.dma_start(out, total[:])

import concourse.mybir as mybir
from concourse.masks import make_identity

C = 128
S = 256
K = 8
N = K * S
K_TENSOR = K - 2
COLS = S // 16

BF16, F32, U16 = mybir.dt.bfloat16, mybir.dt.float32, mybir.dt.uint16
MULT, ADD, NOT_EQUAL = mybir.AluOpType.mult, mybir.AluOpType.add, mybir.AluOpType.not_equal


def cut(parts):
    return [(h * (S // parts), S // parts) for h in range(parts)]


def spread_cuts(p):
    return cut(2 if p == 0 else 1)


def tile_permutedsparseweight_kernel(tc, x, c1, c0, offs, out):
    nc = tc.nc
    with (
        tc.tile_pool(name="held", bufs=1) as held,
        tc.tile_pool(name="pieces", bufs=K) as pieces,
        tc.psum_pool(name="spread_banks", bufs=6) as spread_banks,
        tc.psum_pool(name="sum_bank", bufs=1) as sum_bank,
    ):
        c1_rows = held.tile([C, S], BF16, name="c1_rows")
        nc.sync.dma_start(c1_rows[C - K : C, :], c1.rearrange("o (p s) -> (o p) s", p=K))
        offsets = held.tile([C, N // 16], U16, name="offsets")
        nc.sync.dma_start(offsets[:], offs)
        x_bf16 = held.tile([C, S], BF16, name="x_bf16")
        nc.scalar.dma_start(x_bf16[:], x)
        gain = held.tile([C, 1], F32, name="gain")
        nc.scalar.dma_start(gain[:], c0)

        scratch = held.tile([C, 1], F32, name="scratch")
        nc.vector.memset(scratch[:], 0.0)
        nc.scalar.mul(scratch[:], scratch[:], 1.0)
        nc.vector.memset(c1_rows[0 : C - K, :], 0.0)

        pick = held.tile([C, K], BF16, name="pick")
        nc.gpsimd.memset(pick[:], 0.0)
        nc.gpsimd.affine_select(
            out=pick[:],
            in_=pick[:],
            compare_op=NOT_EQUAL,
            fill=1.0,
            base=K - C,
            pattern=[[-1, K]],
            channel_multiplier=1,
        )

        identity = held.tile([C, C], F32, name="identity")
        make_identity(nc, identity[:])

        window = held.tile([C, S], F32, name="window")
        nc.vector.tensor_copy(window[:], x_bf16[:])

        coefs = []
        for p in range(K):
            coef = pieces.tile([C, S], F32, name="coef")
            coefs.append(coef)
            for first, width in spread_cuts(p):
                columns = slice(first, first + width)
                spread = spread_banks.tile([C, width], F32, name="spread")
                nc.tensor.matmul(
                    spread[:], pick[:, p : p + 1].to_broadcast([C, C]), c1_rows[:, columns], start=True, stop=True
                )
                if p == 0 and first == 0:
                    nc.vector.tensor_copy(coef[:, columns], spread[:])
                else:
                    nc.scalar.mul(coef[:, columns], spread[:], 1.0 if p < K_TENSOR else gain[:, 0:1])

        partial = sum_bank.tile([C, S], F32, name="partial")
        scaled = held.tile([C, S], F32, name="scaled")
        products = []
        for p in range(K):
            product = pieces.tile([C, S], F32, name="product")
            products.append(product)
            for first, width in spread_cuts(p):
                columns = slice(first, first + width)
                picked = window[:].indirect(offsets[:, p * COLS + first // 16 : p * COLS + (first + width) // 16])
                nc.vector.tensor_tensor(product[:, columns], picked, coefs[p][:, columns], MULT)
            if p < K_TENSOR:
                nc.tensor.matmul(partial[:], identity[:], product[:], start=(p == 0), stop=(p == K_TENSOR - 1))

        total = held.tile([C, S], F32, name="total")
        for first, width in cut(2):
            columns = slice(first, first + width)
            nc.vector.scalar_tensor_tensor(
                scaled[:, columns], partial[:, columns], gain[:, 0:1], products[K - 2][:, columns], MULT, ADD
            )
        for first, width in cut(2):
            columns = slice(first, first + width)
            nc.vector.tensor_tensor(total[:, columns], scaled[:, columns], products[K - 1][:, columns], ADD)
        nc.sync.dma_start(out, total[:])
